import numpy as np
import ml_dtypes


def mxq(x, axis, fmt="e4m3"):
    dtype, down = {"e4m3": (ml_dtypes.float8_e4m3fn, 7), "e5m2": (ml_dtypes.float8_e5m2, 14)}[fmt]
    v = np.moveaxis(np.asarray(x, np.float32).astype(ml_dtypes.bfloat16).astype(np.float64), axis, -1)
    blocks = v.reshape(v.shape[:-1] + (-1, 32))
    amax = np.abs(blocks).max(-1, keepdims=True)
    byte = np.maximum(np.where(amax > 0, np.frexp(amax)[1] - 1 + 127, 0) - down, 1)
    scale = np.exp2(byte - 127.0)
    codes = (blocks / scale).astype(np.float32).astype(dtype).astype(np.float64)
    return np.moveaxis((codes * scale).reshape(v.shape), -1, axis)


WIDE = False


def mx_kscale(k):
    if not WIDE:
        return np.ones(k)
    levels = np.array([18, -18])
    if k % 512:
        return np.exp2(np.random.permutation(np.resize(levels, k // 32))).repeat(32)
    a = np.empty((k // 512, 16))
    for p in range(k // 512):
        a[p, :8] = np.random.permutation(np.resize(levels, 8))
        for g in range(8):
            far = levels[np.abs(levels - a[p, g]) >= 10]
            a[p, g + 8] = far[np.random.randint(len(far))]
    return np.exp2(a.ravel()).repeat(32)


BF16 = ml_dtypes.bfloat16


def bf(x):
    return np.asarray(x, np.float32).astype(BF16)


def f64(x):
    return np.asarray(x).astype(np.float64)


T, D, F1, F2 = 1024, 512, 2048, 512
EPS = 1e-3
C = 0.7978845608028654


def _gelu_tanh_grad(z):
    th = np.tanh(C * (z + 0.044715 * z * z * z))
    return 0.5 * (1.0 + th) + 0.5 * z * (1.0 - th * th) * C * (1.0 + 3.0 * 0.044715 * z * z)


def setup_inputs():
    s = np.maximum(mx_kscale(T), 1.0)[:, None]
    u = mx_kscale(F2)
    v = mx_kscale(F1)
    x0 = bf(np.random.standard_normal((T, D)) + 0.5)
    gamma = bf(1.0 + 0.1 * np.random.standard_normal(D))
    beta = bf(0.1 * np.random.standard_normal(D))
    w1_0 = bf(np.random.standard_normal((D, F1)) / np.sqrt(D))
    b1 = bf(0.1 * np.random.standard_normal(F1))
    w2_0 = bf(np.random.standard_normal((F1, F2)) * 1.5 / np.sqrt(F1))
    b2 = bf(0.1 * np.random.standard_normal(F2))
    g = bf(np.random.standard_normal((T, F2)) * np.exp2(np.random.randint(-6, 1, (T, 1))) / s * u)
    xf = f64(x0)
    mu = np.mean(xf, axis=-1, keepdims=True)
    rstd = 1.0 / np.sqrt(np.mean(np.square(xf - mu), axis=-1, keepdims=True) + EPS)
    z1 = ((xf - mu) * rstd * f64(gamma) + f64(beta)) @ f64(w1_0) + f64(b1)
    return {"inputs": bf(f64(x0) * s), "gamma": gamma, "beta": beta,
            "fc1_kernel": bf(f64(w1_0) / v), "fc1_bias": b1,
            "fc2_kernel": bf(f64(w2_0) * v[:, None] / u), "fc2_bias": b2,
            "mu": np.asarray(mu, np.float32), "rstd": np.asarray(rstd, np.float32), "z1": np.asarray(z1, np.float32),
            "grad_out": g}


def reference(inputs, gamma, beta, fc1_kernel, fc1_bias, fc2_kernel, fc2_bias, mu, rstd, z1, grad_out):
    gf, r = f64(gamma), f64(rstd)
    xhat = (f64(inputs) - f64(mu)) * r
    ln = xhat * gf + f64(beta)
    dh = mxq(f64(grad_out), 1, "e5m2") @ mxq(f64(fc2_kernel), 1, "e4m3").T
    dz1 = dh * _gelu_tanh_grad(f64(z1))
    dln = mxq(dz1, 1, "e5m2") @ mxq(f64(fc1_kernel), 1, "e4m3").T
    dw1 = mxq(ln, 0, "e4m3").T @ mxq(dz1, 0, "e5m2")
    dxhat = dln * gf
    m1 = np.mean(dxhat, axis=-1, keepdims=True)
    m2 = np.mean(dxhat * xhat, axis=-1, keepdims=True)
    dx = r * (dxhat - m1 - xhat * m2)
    return dx, dw1

@@ -1,0 +1,563 @@
+import math
+from contextlib import ExitStack
+from functools import partial
+
+import concourse.mybir as mybir
+from concourse.masks import make_identity
+
+T, D, F1, F2 = 1024, 512, 2048, 512
+FLOPS = 2 * T * F2 * F1 + 2 * T * F1 * D + 2 * T * D * F1
+BYTES = 2 * (T * D + 2 * D + D * F1 + F1 * F2 + T * F2) + 4 * (2 * T + T * F1 + T * D + D * F1)
+
+F32 = mybir.dt.float32
+BF16 = mybir.dt.bfloat16
+U32 = mybir.dt.uint32
+U8 = mybir.dt.uint8
+E4M3 = mybir.dt.float8_e4m3fn_x4
+E5M2 = mybir.dt.float8_e5m2_x4
+ALU = mybir.AluOpType
+ACT = mybir.ActivationFunctionType
+
+P = 128
+PACK = 4
+K_PASS = P * PACK
+HALVES = T // K_PASS
+CHUNKS = F1 // K_PASS
+UNITS = HALVES * CHUNKS
+GELU_C = 0.7978845608028654
+GELU_A = 0.044715
+EARLY = 3
+DH_BANKS = 3
+SIDE_BANKS = 5
+
+
+def tile_layernormmlp_v_kernel(
+    tc, inputs, gamma, beta, fc1_kernel, fc1_bias, fc2_kernel, fc2_bias, mu, rstd, z1, grad_out, out_0, out_1
+):
+    nc = tc.nc
+    with ExitStack() as ctx:
+        keep = ctx.enter_context(tc.tile_pool(name="keep", bufs=1))
+        work = ctx.enter_context(tc.tile_pool(name="work", bufs=2))
+        psum = ctx.enter_context(tc.psum_pool(name="psum", bufs=2))
+        ctx.enter_context(tc.manual_schedule())
+
+        ident_f32 = keep.tile([P, P], F32)
+        ident_bf16 = keep.tile([P, P], BF16)
+        affine_rows = keep.tile([P, P], BF16)
+        affine_cols = keep.tile([P, 2 * PACK], F32)
+        gamma_row = keep.tile([P, D], F32)
+        mu_sb = keep.tile([P, HALVES, PACK], F32)
+        rstd_sb = keep.tile([P, HALVES, PACK], F32)
+        sums = keep.tile([P, HALVES * PACK, 2], F32)
+        xhat = [keep.tile([P, PACK, D], F32, name="xhat%d" % g) for g in range(HALVES)]
+
+        def mx_operand(pool, tag, bufs):
+            codes = pool.tile([P, K_PASS], U32, name=tag + "_codes", bufs=bufs, align_bytes=64)
+            scales = pool.tile([P, K_PASS], U8, name=tag + "_scales", bufs=bufs, align_bytes=64)
+            return codes, scales
+
+        def quantize(operand, staged, fmt, first=0, count=PACK):
+            codes, scales = operand
+            cols = slice(first * P, (first + count) * P)
+            nc.vector.quantize_mx(
+                out=codes[:, cols].bitcast(fmt),
+                scales=scales[:, cols],
+                in_=staged[:, first * K_PASS : (first + count) * K_PASS],
+            )
+
+        def mx_pass(bank, still, still_fmt, block, moving, moving_fmt, start, stop):
+            cols = slice(block * P, (block + 1) * P)
+            nc.tensor.matmul_mx(
+                out=bank[:],
+                lhsT=still[0][:, cols].bitcast(still_fmt),
+                lhsT_scale=still[1][:, cols],
+                rhs=moving[0][:].bitcast(moving_fmt),
+                rhs_scale=moving[1][:],
+                start=start,
+                stop=stop,
+            )
+
+        def new_staged(tag, bufs):
+            return work.tile([P, PACK * K_PASS], BF16, name=tag, bufs=bufs, align_bytes=64)
+
+        def side_bank():
+            return psum.tile([P, K_PASS], F32, name="side", bufs=SIDE_BANKS)
+
+        def turn_words(bank, word_block):
+            for b in range(2):
+                for u in range(2):
+                    s = 2 * b + u
+                    nc.tensor.transpose(bank[:, s * P : (s + 1) * P], word_block(b, u), ident_f32[:])
+
+        def collect_words(copy, staged, pair, bank):
+            words = staged[:].bitcast(F32)[:, pair * K_PASS : (pair + 1) * K_PASS]
+            copy(
+                out=words.rearrange("p (b r u) -> p b r u", b=2, u=2),
+                in_=bank[:].rearrange("p (b u r) -> p b r u", b=2, u=2),
+            )
+
+        raw = {}
+
+        def load_raw(key, rows):
+            raw[key] = work.tile([P, PACK, K_PASS], BF16, name="raw", bufs=5)
+            nc.sync.dma_start(out=raw[key][:], in_=rows)
+
+        def token_rows(src, g):
+            return src[g * K_PASS : (g + 1) * K_PASS, :].rearrange("(p j) w -> p j w", j=PACK)
+
+        def load_grad(g):
+            load_raw(("g", g), token_rows(grad_out, g))
+
+        def load_x(g):
+            load_raw(("x", g), token_rows(inputs, g))
+
+        def load_w2(c):
+            load_raw(("w2", c), fc2_kernel[c * K_PASS : (c + 1) * K_PASS, :].rearrange("(m p) k -> p m k", p=P))
+
+        def load_w1(c):
+            load_raw(("w1", c), fc1_kernel[:, c * K_PASS : (c + 1) * K_PASS].rearrange("(m p) k -> p m k", p=P))
+
+        staged_of = {}
+        mx = {}
+
+        def turn_raw(key, copy):
+            words = raw[key][:].rearrange("p m k -> p (m k)").bitcast(F32)
+
+            def fill(pair):
+                bank = side_bank()
+                turn_words(
+                    bank, lambda b, u: words[:, (2 * pair + b) * 2 * P + u : (2 * pair + b + 1) * 2 * P : 2]
+                )
+                return bank
+
+            def drain(pair, bank):
+                if pair == 0:
+                    staged_of[key] = new_staged("side_staged", 2)
+                collect_words(copy, staged_of[key], pair, bank)
+
+            return [(partial(fill, pair), partial(drain, pair)) for pair in range(2)]
+
+        def quantize_raw(key, fmt):
+            mx[key] = mx_operand(keep, "%s%d" % key, 1)
+            quantize(mx[key], staged_of[key], fmt)
+
+        z_sb, sq, gate, tanh_sb, dz = {}, {}, {}, {}, {}
+        dh = {}
+
+        def load_z(n, pieces):
+            c, g = divmod(n, HALVES)
+            if n not in z_sb:
+                z_sb[n] = work.tile([P, PACK, K_PASS], F32, name="z", tag="z", bufs=3)
+            rows = token_rows(z1, g)
+            for js in pieces:
+                nc.sync.dma_start(out=z_sb[n][:, js, :], in_=rows[:, js, c * K_PASS : (c + 1) * K_PASS])
+
+        def square(n, js):
+            if n not in sq:
+                sq[n] = work.tile([P, PACK, K_PASS], F32, name="sq", tag="sq", bufs=2)
+            nc.scalar.activation(
+                out=sq[n][:, js, :], in_=z_sb[n][:, js, :], func=ACT.Square, scale=math.sqrt(3.0 * GELU_A * GELU_C)
+            )
+
+        def gelu_neg(n, js):
+            if n not in gate:
+                gate[n] = work.tile([P, PACK, K_PASS], F32, name="gate", bufs=3)
+            nc.scalar.activation(out=gate[n][:, js, :], in_=z_sb[n][:, js, :], func=ACT.Gelu_apprx_tanh, scale=-1.0)
+
+        def cubic(n, js):
+            if n not in tanh_sb:
+                tanh_sb[n] = work.tile([P, PACK, K_PASS], F32, name="tanh_sb", bufs=2)
+            nc.vector.scalar_tensor_tensor(
+                out=tanh_sb[n][:, js, :], in0=sq[n][:, js, :], scalar=3.0 * GELU_C, in1=z_sb[n][:, js, :],
+                op0=ALU.add, op1=ALU.mult,
+            )
+
+        def tanh_neg(n, js):
+            nc.scalar.activation(out=tanh_sb[n][:, js, :], in_=tanh_sb[n][:, js, :], func=ACT.Tanh, scale=-1.0 / 3.0)
+
+        def slope(n, js):
+            nc.vector.scalar_tensor_tensor(
+                out=gate[n][:, js, :], in0=sq[n][:, js, :], scalar=GELU_C, in1=gate[n][:, js, :],
+                op0=ALU.add, op1=ALU.mult,
+            )
+
+        def dh_pass(n, j):
+            c, g = divmod(n, HALVES)
+            dh[n, j] = dh_bank()
+            mx_pass(dh[n, j], mx["g", g], E5M2, j, mx["w2", c], E4M3, True, True)
+
+        def take_dh(n, j):
+            nc.vector.scalar_tensor_tensor(
+                out=tanh_sb[n][:, j, :], in0=tanh_sb[n][:, j, :], scalar=1.0, in1=dh[n, j][:],
+                op0=ALU.subtract, op1=ALU.mult,
+            )
+
+        def round_dz(n, js):
+            if n not in dz:
+                dz[n] = work.tile([P, 2, PACK, 2 * P], BF16, name="dz", bufs=2)
+            for u in range(2):
+                nc.vector.scalar_tensor_tensor(
+                    out=dz[n][:, u, js, :].rearrange("p j (m e) -> p (j m) e", e=2),
+                    in0=gate[n][:, js, :].rearrange("p j (m u e) -> p (j m) u e", u=2, e=2)[:, :, u, :],
+                    scalar=0.5,
+                    in1=tanh_sb[n][:, js, :].rearrange("p j (m u e) -> p (j m) u e", u=2, e=2)[:, :, u, :],
+                    op0=ALU.subtract, op1=ALU.mult,
+                )
+
+        feat_bank, tok_bank = {}, {}
+
+        def turn_dz(n, pair):
+            words = dz[n][:].rearrange("p u j x -> p (u j x)").bitcast(F32)
+            feat_bank[n, pair] = side_bank()
+            turn_words(
+                feat_bank[n, pair],
+                lambda b, u: words[:, (u * PACK + 2 * pair + b) * P : (u * PACK + 2 * pair + b + 1) * P],
+            )
+
+        def weave_dz(n, u):
+            tok_bank[n, u] = psum.tile([P, 2 * K_PASS], BF16, name="side", bufs=SIDE_BANKS)
+            for h in range(2):
+                nc.tensor.matmul(
+                    out=tok_bank[n, u][:, h * K_PASS : (h + 1) * K_PASS].rearrange("p (f j) -> p f j", j=PACK),
+                    lhsT=ident_bf16[:],
+                    rhs=dz[n][:, u, :, h * P : (h + 1) * P].rearrange("p j f -> p f j"),
+                    start=True,
+                    stop=True,
+                )
+
+        def collect_feat(n, pair):
+            if ("feat", n) not in staged_of:
+                staged_of["feat", n] = new_staged("dz_staged", 3)
+            collect_words(nc.scalar.copy, staged_of["feat", n], pair, feat_bank[n, pair])
+
+        def collect_tok(n, u):
+            if ("tok", n) not in staged_of:
+                staged_of["tok", n] = new_staged("dz_staged", 3)
+            nc.scalar.copy(out=staged_of["tok", n][:, u * 2 * K_PASS : (u + 1) * 2 * K_PASS], in_=tok_bank[n, u][:])
+
+        def quantize_feat(n, first, count):
+            if ("feat", n) not in mx:
+                mx["feat", n] = mx_operand(work, "feat", 8)
+            quantize(mx["feat", n], staged_of["feat", n], E5M2, first, count)
+
+        def quantize_tok(n):
+            mx["tok", n] = mx_operand(work, "tok", 6)
+            quantize(mx["tok", n], staged_of["tok", n], E5M2)
+
+        def normalise(g):
+            for j in range(PACK):
+                nc.vector.tensor_scalar(
+                    out=xhat[g][:, j, :], in0=raw["x", g][:, j, :],
+                    scalar1=mu_sb[:, g, j : j + 1], scalar2=rstd_sb[:, g, j : j + 1],
+                    op0=ALU.subtract, op1=ALU.mult,
+                )
+
+        ln_t = {}
+
+        def ln_blocks(g):
+            def fill(m):
+                bank = side_bank()
+                for j in range(PACK):
+                    nc.tensor.transpose(
+                        bank[:, j * P : (j + 1) * P], xhat[g][:, j, m * P : (m + 1) * P], ident_f32[:]
+                    )
+                return bank
+
+            def drain(m, bank):
+                ln_t[g, m] = work.tile([P, K_PASS], BF16, name="ln_t", bufs=4)
+                nc.scalar.activation(
+                    out=ln_t[g, m][:].rearrange("p (u r e) -> p u r e", u=2, e=2),
+                    in_=bank[:].rearrange("p (u e r) -> p u r e", u=2, e=2),
+                    func=ACT.Identity,
+                    scale=affine_cols[:, m : m + 1],
+                    bias=affine_cols[:, PACK + m : PACK + m + 1],
+                )
+
+            return [(partial(fill, m), partial(drain, m)) for m in range(PACK)]
+
+        def ln_turns(g):
+            def fill(pair):
+                bank = side_bank()
+                turn_words(bank, lambda b, u: ln_t[g, 2 * pair + b][:].bitcast(F32)[:, u * P : (u + 1) * P])
+                return bank
+
+            def drain(pair, bank):
+                if pair == 0:
+                    staged_of["ln", g] = new_staged("side_staged", 2)
+                collect_words(nc.scalar.copy, staged_of["ln", g], pair, bank)
+
+            return [(partial(fill, pair), partial(drain, pair)) for pair in range(2)]
+
+        def dw_blocks(c):
+            def fill(m):
+                bank = side_bank()
+                for g in range(HALVES):
+                    mx_pass(bank, mx["ln", g], E4M3, m, mx["tok", c * HALVES + g], E5M2, g == 0, g == HALVES - 1)
+                return bank
+
+            def drain(m, bank):
+                dw = work.tile([P, K_PASS], F32, name="dw", bufs=8)
+                nc.scalar.copy(
+                    out=dw[:].rearrange("p (m u e) -> p m u e", u=2, e=2),
+                    in_=bank[:].rearrange("p (u m e) -> p m u e", u=2, e=2),
+                )
+                nc.sync.dma_start(out=out_1[m * P : (m + 1) * P, c * K_PASS : (c + 1) * K_PASS], in_=dw[:])
+
+            return [(partial(fill, m), partial(drain, m)) for m in range(PACK)]
+
+        def start_jobs(jobs, lead):
+            return [fill() for fill, drain in jobs[:lead]]
+
+        def finish_jobs(jobs, banks):
+            lead = len(banks)
+            for k, (fill, drain) in enumerate(jobs):
+                drain(banks[k])
+                if k + lead < len(jobs):
+                    banks.append(jobs[k + lead][0]())
+
+        def run_jobs(jobs, lead):
+            finish_jobs(jobs, start_jobs(jobs, lead))
+
+        scaled, dx, scaled_sb, dx_sb = {}, {}, {}, {}
+
+        dln = {}
+
+        def dln_passes(g, j, chunks, bank=None):
+            if (g, j) not in dln:
+                dln[g, j] = bank
+            for c in chunks:
+                mx_pass(dln[g, j], mx["feat", c * HALVES + g], E5M2, j, mx["w1", c], E4M3, c == 0, c == CHUNKS - 1)
+            return dln[g, j]
+
+        def take_dln(g, j, bank):
+            if j == 0:
+                scaled_sb[g] = work.tile([P, PACK, D], F32, name="scaled", tag="sq", bufs=2)
+            scaled[g, j] = scaled_sb[g][:, j, :]
+            nc.vector.scalar_tensor_tensor(
+                out=scaled[g, j], in0=bank[:], scalar=rstd_sb[:, g, j : j + 1], in1=gamma_row[:],
+                op0=ALU.mult, op1=ALU.mult, accum_out=sums[:, g * PACK + j, 0:1],
+            )
+
+        def dln_jobs(g, js):
+            return [(lambda j=j: dln_passes(g, j, range(CHUNKS), side_bank()), partial(take_dln, g, j)) for j in js]
+
+        def dx_moment(g, j):
+            if j == 0:
+                dx_sb[g] = work.tile([P, PACK, D], F32, name="dx", tag="z", bufs=3)
+            dx[g, j] = dx_sb[g][:, j, :]
+            nc.vector.scalar_tensor_tensor(
+                out=dx[g, j], in0=scaled[g, j], scalar=1.0, in1=xhat[g][:, j, :],
+                op0=ALU.mult, op1=ALU.mult, accum_out=sums[:, g * PACK + j, 1:2],
+            )
+
+        def dx_shift(g, j):
+            nc.scalar.activation(
+                out=dx[g, j], in_=xhat[g][:, j, :], func=ACT.Identity,
+                scale=sums[:, g * PACK + j, 1:2], bias=sums[:, g * PACK + j, 0:1],
+            )
+
+        def dx_finish(g, j):
+            nc.vector.scalar_tensor_tensor(
+                out=dx[g, j], in0=dx[g, j], scalar=-1.0 / D, in1=scaled[g, j], op0=ALU.mult, op1=ALU.add
+            )
+            nc.sync.dma_start(out=token_rows(out_0, g)[:, j, :], in_=dx[g, j])
+
+        whole = slice(0, PACK)
+        singles = [slice(j, j + 1) for j in range(PACK)]
+        pairs = [slice(0, 2), slice(2, 4)]
+
+        def affine_jobs():
+            def fill_cols():
+                bank = psum.tile([P, P], BF16, name="side", bufs=SIDE_BANKS)
+                nc.tensor.transpose(bank[:], affine_rows[:], ident_bf16[:])
+                return bank
+
+            def fill_row():
+                bank = side_bank()
+                for m in range(PACK):
+                    nc.tensor.transpose(
+                        bank[:, m * P : (m + 1) * P], affine_cols[:, m : m + 1].to_broadcast([P, P]), ident_f32[:]
+                    )
+                return bank
+
+            return [
+                (fill_cols, lambda bank: nc.scalar.copy(out=affine_cols[:], in_=bank[:, 0 : 2 * PACK])),
+                (fill_row, lambda bank: nc.scalar.copy(out=gamma_row[:], in_=bank[:])),
+            ]
+
+        def dh_bank():
+            return psum.tile([P, K_PASS], F32, name="dh", bufs=DH_BANKS)
+
+        make_identity(nc, ident_f32[:])
+        nc.gpsimd.memset(affine_rows[:], 0.0)
+        make_identity(nc, ident_bf16[:])
+        load_z(0, singles[:1])
+        load_grad(0)
+        load_z(0, singles[1:2])
+        load_w2(0)
+        load_z(0, pairs[1:])
+        load_z(1, [whole])
+        load_grad(1)
+        load_x(0)
+        nc.sync.dma_start(out=affine_rows[0:PACK, :], in_=gamma.rearrange("(m p) -> m p", p=P))
+        nc.sync.dma_start(out=affine_rows[PACK : 2 * PACK, :], in_=beta.rearrange("(m p) -> m p", p=P))
+        nc.sync.dma_start(out=mu_sb[:], in_=mu.rearrange("(g p j) o -> p g (j o)", g=HALVES, j=PACK))
+        nc.sync.dma_start(out=rstd_sb[:], in_=rstd.rearrange("(g p j) o -> p g (j o)", g=HALVES, j=PACK))
+        load_z(2, [whole])
+
+        head_jobs = turn_raw(("g", 0), nc.vector.tensor_copy) + turn_raw(("w2", 0), nc.vector.tensor_copy)
+        banks = start_jobs(head_jobs, 4)
+        gelu_neg(0, singles[0])
+        for js in singles[:2]:
+            square(0, js)
+            cubic(0, js)
+        gelu_neg(0, singles[1])
+        finish_jobs(head_jobs[:2], banks[:2])
+        square(0, pairs[1])
+        tanh_neg(0, pairs[0])
+        cubic(0, pairs[1])
+        gelu_neg(0, pairs[1])
+        tanh_neg(0, pairs[1])
+        finish_jobs(head_jobs[2:], banks[2:])
+        quantize_raw(("g", 0), E5M2)
+        quantize_raw(("w2", 0), E4M3)
+        slope(0, whole)
+        square(1, whole)
+        for j in range(DH_BANKS):
+            dh_pass(0, j)
+
+        loads = {
+            -1: [partial(load_w1, 0), partial(load_w1, 1), partial(load_w2, 1)],
+            0: [partial(load_w1, 2)],
+            1: [partial(load_w2, 2), partial(load_w1, 3)],
+            2: [partial(load_x, 1)],
+            3: [partial(load_w2, 3)],
+        }
+        operands = {
+            0: [(("g", 1), E5M2), (("w1", 0), E4M3)],
+            1: [(("w2", 1), E4M3)],
+            2: [(("w1", 1), E4M3)],
+            3: [(("w2", 2), E4M3), (("w1", 2), E4M3)],
+            4: [(("w1", 3), E4M3)],
+            5: [(("w2", 3), E4M3)],
+        }
+        for step in loads[-1]:
+            step()
+
+        for n in range(UNITS - 1):
+            jobs = []
+            if n == 0:
+                jobs = jobs + affine_jobs()[:1]
+            if n == 6:
+                jobs = jobs + affine_jobs()[1:]
+            for key, fmt in operands.get(n, []):
+                jobs = jobs + turn_raw(key, nc.scalar.copy)
+            if n in (2, 5):
+                jobs = jobs + ln_turns(n // 3)
+            if n in (1, 4):
+                jobs = jobs + ln_blocks(n // 3)
+            if n == 6:
+                jobs = jobs + dw_blocks(0) + dw_blocks(1)
+            gelu_neg(n + 1, whole)
+            cubic(n + 1, whole)
+            if n + 3 < UNITS:
+                load_z(n + 3, [whole])
+            banks = start_jobs(jobs, EARLY)
+            take_dh(n, 0)
+            for j in range(DH_BANKS, PACK):
+                dh_pass(n, j)
+            if n > 0:
+                for k in range(2):
+                    collect_tok(n - 1, k)
+            banks = banks + start_jobs(jobs[EARLY:], SIDE_BANKS - EARLY)
+            for j in range(1, PACK):
+                take_dh(n, j)
+            tanh_neg(n + 1, whole)
+            finish_jobs(jobs, banks)
+            if n > 0:
+                quantize_feat(n - 1, 0, PACK)
+                quantize_tok(n - 1)
+            ready = ("g", (n + 1) % HALVES) in mx and ("w2", (n + 1) // HALVES) in mx
+            if ready:
+                for j in range(DH_BANKS):
+                    dh_pass(n + 1, j)
+            round_dz(n, whole)
+            for k in range(2):
+                turn_dz(n, k)
+            for k in range(2):
+                weave_dz(n, k)
+            if n + 2 < UNITS:
+                square(n + 2, whole)
+            for key, fmt in operands.get(n, []):
+                quantize_raw(key, fmt)
+            if n in (2, 5):
+                quantize_raw(("ln", n // 3), E4M3)
+            slope(n + 1, whole)
+            if n in (0, 3):
+                normalise(n // 3)
+            if not ready:
+                for j in range(DH_BANKS):
+                    dh_pass(n + 1, j)
+            for k in range(2):
+                collect_feat(n, k)
+            for step in loads.get(n, []):
+                step()
+
+        n = UNITS - 1
+        take_dh(n, 0)
+        for j in range(DH_BANKS, PACK):
+            dh_pass(n, j)
+        for k in range(2):
+            collect_tok(n - 1, k)
+        take_dh(n, 1)
+        quantize_feat(n - 1, 0, PACK)
+        take_dh(n, 2)
+        take_dh(n, 3)
+        quantize_tok(n - 1)
+        for j in range(DH_BANKS):
+            dln_passes(0, j, range(CHUNKS), dh_bank())
+        round_dz(n, whole)
+        for k in range(2):
+            turn_dz(n, k)
+        dln_passes(0, 3, range(CHUNKS), side_bank())
+        for k in range(2):
+            weave_dz(n, k)
+        for k in range(2):
+            collect_feat(n, k)
+        for k in range(2):
+            collect_tok(n, k)
+        for j in range(PACK):
+            take_dln(0, j, dln[0, j])
+        jobs = dw_blocks(2) + dw_blocks(3)
+        banks = start_jobs(jobs[:4], 4)
+        quantize_feat(n, 0, PACK)
+        for j in range(DH_BANKS):
+            dln_passes(1, j, range(CHUNKS), dh_bank())
+        for j in range(2):
+            dx_moment(0, j)
+            dx_shift(0, j)
+        quantize_tok(n)
+        finish_jobs(jobs[:2], banks[:2])
+        for j in range(2, 4):
+            dx_moment(0, j)
+            dx_shift(0, j)
+        finish_jobs(jobs[2:4], banks[2:])
+        banks = start_jobs(jobs[4:], 4)
+        dx_finish(0, 0)
+        dx_finish(0, 1)
+        take_dln(1, 0, dln[1, 0])
+        dln_passes(1, 3, range(CHUNKS), dh_bank())
+        take_dln(1, 1, dln[1, 1])
+        finish_jobs(jobs[4:], banks)
+        dx_finish(0, 2)
+        dx_finish(0, 3)
+        for j in range(2):
+            dx_moment(1, j)
+            dx_shift(1, j)
+        for j in range(2, 4):
+            take_dln(1, j, dln[1, j])
+        for j in range(2, 4):
+            dx_moment(1, j)
+            dx_shift(1, j)
+        for j in range(PACK):
+            dx_finish(1, j)

@@ -20,15 +20,14 @@ ACT = mybir.ActivationFunctionType
 
 P = 128
 PACK = 4
-K_PASS = P * PACK
-HALVES = T // K_PASS
-CHUNKS = F1 // K_PASS
+WIDE = P * PACK
+HALVES = T // WIDE
+CHUNKS = F1 // WIDE
 UNITS = HALVES * CHUNKS
 GELU_C = 0.7978845608028654
 GELU_A = 0.044715
-EARLY = 3
-DH_BANKS = 3
-SIDE_BANKS = 5
+ROW_BANKS = 4
+TURN_BANKS = 4
 
 
 def tile_layernormmlp_v_kernel(
@@ -38,7 +37,7 @@ def tile_layernormmlp_v_kernel(
     with ExitStack() as ctx:
         keep = ctx.enter_context(tc.tile_pool(name="keep", bufs=1))
         work = ctx.enter_context(tc.tile_pool(name="work", bufs=2))
-        psum = ctx.enter_context(tc.psum_pool(name="psum", bufs=2))
+        psum = ctx.enter_context(tc.psum_pool(name="psum", bufs=ROW_BANKS))
         ctx.enter_context(tc.manual_schedule())
 
         ident_f32 = keep.tile([P, P], F32)
@@ -51,19 +50,15 @@ def tile_layernormmlp_v_kernel(
         sums = keep.tile([P, HALVES * PACK, 2], F32)
         xhat = [keep.tile([P, PACK, D], F32, name="xhat%d" % g) for g in range(HALVES)]
 
-        def mx_operand(pool, tag, bufs):
-            codes = pool.tile([P, K_PASS], U32, name=tag + "_codes", bufs=bufs, align_bytes=64)
-            scales = pool.tile([P, K_PASS], U8, name=tag + "_scales", bufs=bufs, align_bytes=64)
-            return codes, scales
+        raw, staged, mx = {}, {}, {}
+        z_sb, square_sb, slope_sb, tanh_sb, dh, dz, dz_banks = {}, {}, {}, {}, {}, {}, {}
+        ln_t, dln, scaled, dx = {}, {}, {}, {}
 
-        def quantize(operand, staged, fmt, first=0, count=PACK):
-            codes, scales = operand
-            cols = slice(first * P, (first + count) * P)
-            nc.vector.quantize_mx(
-                out=codes[:, cols].bitcast(fmt),
-                scales=scales[:, cols],
-                in_=staged[:, first * K_PASS : (first + count) * K_PASS],
-            )
+        def row_bank():
+            return psum.tile([P, WIDE], F32, name="row_bank", bufs=ROW_BANKS)
+
+        def turn_bank(width=WIDE, dtype=F32):
+            return psum.tile([P, width], dtype, name="turn_bank", bufs=TURN_BANKS)
 
         def mx_pass(bank, still, still_fmt, block, moving, moving_fmt, start, stop):
             cols = slice(block * P, (block + 1) * P)
@@ -71,178 +66,207 @@ def tile_layernormmlp_v_kernel(
                 out=bank[:],
                 lhsT=still[0][:, cols].bitcast(still_fmt),
                 lhsT_scale=still[1][:, cols],
-                rhs=moving[0][:].bitcast(moving_fmt),
-                rhs_scale=moving[1][:],
+                rhs=moving[0].bitcast(moving_fmt),
+                rhs_scale=moving[1],
                 start=start,
                 stop=stop,
             )
 
-        def new_staged(tag, bufs):
-            return work.tile([P, PACK * K_PASS], BF16, name=tag, bufs=bufs, align_bytes=64)
-
-        def side_bank():
-            return psum.tile([P, K_PASS], F32, name="side", bufs=SIDE_BANKS)
-
-        def turn_words(bank, word_block):
+        def turn_words(word_block):
+            bank = turn_bank()
             for b in range(2):
                 for u in range(2):
                     s = 2 * b + u
                     nc.tensor.transpose(bank[:, s * P : (s + 1) * P], word_block(b, u), ident_f32[:])
+            return bank
 
-        def collect_words(copy, staged, pair, bank):
-            words = staged[:].bitcast(F32)[:, pair * K_PASS : (pair + 1) * K_PASS]
+        def collect_words(copy, target, pair, bank):
+            words = target.bitcast(F32)[:, pair * WIDE : (pair + 1) * WIDE]
             copy(
                 out=words.rearrange("p (b r u) -> p b r u", b=2, u=2),
                 in_=bank[:].rearrange("p (b u r) -> p b r u", b=2, u=2),
             )
 
-        raw = {}
+        def fill_jobs(jobs):
+            return [fill() for fill, drain in jobs]
 
-        def load_raw(key, rows):
-            raw[key] = work.tile([P, PACK, K_PASS], BF16, name="raw", bufs=5)
-            nc.sync.dma_start(out=raw[key][:], in_=rows)
+        def drain_jobs(jobs, banks):
+            banks = list(banks)
+            for k, (fill, drain) in enumerate(jobs):
+                drain(banks[k])
+                if len(banks) < len(jobs):
+                    banks.append(jobs[len(banks)][0]())
 
         def token_rows(src, g):
-            return src[g * K_PASS : (g + 1) * K_PASS, :].rearrange("(p j) w -> p j w", j=PACK)
+            return src[g * WIDE : (g + 1) * WIDE, :].rearrange("(p j) w -> p j w", j=PACK)
 
-        def load_grad(g):
-            load_raw(("g", g), token_rows(grad_out, g))
+        def load_raw(key):
+            kind, i = key
+            cut = slice(i * WIDE, (i + 1) * WIDE)
+            if kind == "grad":
+                rows = token_rows(grad_out, i)
+            elif kind == "x":
+                rows = token_rows(inputs, i)
+            elif kind == "w2":
+                rows = fc2_kernel[cut, :].rearrange("(m p) k -> p m k", p=P)
+            else:
+                rows = fc1_kernel[:, cut].rearrange("(m p) k -> p m k", p=P)
+            raw[key] = work.tile([P, PACK, WIDE], BF16, name="raw", bufs=4)
+            nc.sync.dma_start(out=raw[key][:], in_=rows)
 
-        def load_x(g):
-            load_raw(("x", g), token_rows(inputs, g))
-
-        def load_w2(c):
-            load_raw(("w2", c), fc2_kernel[c * K_PASS : (c + 1) * K_PASS, :].rearrange("(m p) k -> p m k", p=P))
-
-        def load_w1(c):
-            load_raw(("w1", c), fc1_kernel[:, c * K_PASS : (c + 1) * K_PASS].rearrange("(m p) k -> p m k", p=P))
-
-        staged_of = {}
-        mx = {}
-
-        def turn_raw(key, copy):
-            words = raw[key][:].rearrange("p m k -> p (m k)").bitcast(F32)
-
-            def fill(pair):
-                bank = side_bank()
-                turn_words(
-                    bank, lambda b, u: words[:, (2 * pair + b) * 2 * P + u : (2 * pair + b + 1) * 2 * P : 2]
-                )
-                return bank
-
-            def drain(pair, bank):
-                if pair == 0:
-                    staged_of[key] = new_staged("side_staged", 2)
-                collect_words(copy, staged_of[key], pair, bank)
-
-            return [(partial(fill, pair), partial(drain, pair)) for pair in range(2)]
-
-        def quantize_raw(key, fmt):
-            mx[key] = mx_operand(keep, "%s%d" % key, 1)
-            quantize(mx[key], staged_of[key], fmt)
-
-        z_sb, sq, gate, tanh_sb, dz = {}, {}, {}, {}, {}
-        dh = {}
-
-        def load_z(n, pieces):
+        def load_z(n, rows=slice(0, PACK), cols=slice(0, WIDE)):
             c, g = divmod(n, HALVES)
             if n not in z_sb:
-                z_sb[n] = work.tile([P, PACK, K_PASS], F32, name="z", tag="z", bufs=3)
-            rows = token_rows(z1, g)
-            for js in pieces:
-                nc.sync.dma_start(out=z_sb[n][:, js, :], in_=rows[:, js, c * K_PASS : (c + 1) * K_PASS])
+                z_sb[n] = work.tile([P, PACK, WIDE], F32, name="z", tag="z", bufs=3)
+            unit = token_rows(z1, g)[:, :, c * WIDE : (c + 1) * WIDE]
+            nc.sync.dma_start(out=z_sb[n][:, rows, cols], in_=unit[:, rows, cols])
 
-        def square(n, js):
-            if n not in sq:
-                sq[n] = work.tile([P, PACK, K_PASS], F32, name="sq", tag="sq", bufs=2)
+        def collect_operand(key, copy, pair, bank):
+            if pair == 0:
+                staged[key] = work.tile([P, PACK * WIDE], BF16, name="staged", bufs=3, align_bytes=64)
+            collect_words(copy, staged[key][:], pair, bank)
+
+        def operand_jobs(key, copy):
+            words = raw[key][:].rearrange("p m k -> p (m k)").bitcast(F32)
+
+            def word_block(pair, b, u):
+                row = 2 * pair + b
+                return words[:, row * 2 * P + u : (row + 1) * 2 * P : 2]
+
+            return [
+                (partial(turn_words, partial(word_block, pair)), partial(collect_operand, key, copy, pair))
+                for pair in range(2)
+            ]
+
+        def quantize_operand(key):
+            codes = keep.tile([P, WIDE], U32, name="%s%d_codes" % key, align_bytes=64)
+            scales = keep.tile([P, WIDE], U8, name="%s%d_scales" % key, align_bytes=64)
+            mx[key] = (codes[:], scales[:])
+            fmt = E5M2 if key[0] == "grad" else E4M3
+            nc.vector.quantize_mx(out=codes[:].bitcast(fmt), scales=scales[:], in_=staged[key][:])
+
+        whole = (slice(0, P), slice(0, PACK), slice(0, WIDE))
+
+        def square(n, part=whole):
+            if n not in square_sb:
+                square_sb[n] = work.tile([P, PACK, WIDE], F32, name="square", tag="square", bufs=2)
             nc.scalar.activation(
-                out=sq[n][:, js, :], in_=z_sb[n][:, js, :], func=ACT.Square, scale=math.sqrt(3.0 * GELU_A * GELU_C)
+                out=square_sb[n][part], in_=z_sb[n][part], func=ACT.Square, scale=math.sqrt(3.0 * GELU_A * GELU_C)
             )
 
-        def gelu_neg(n, js):
-            if n not in gate:
-                gate[n] = work.tile([P, PACK, K_PASS], F32, name="gate", bufs=3)
-            nc.scalar.activation(out=gate[n][:, js, :], in_=z_sb[n][:, js, :], func=ACT.Gelu_apprx_tanh, scale=-1.0)
+        def gelu_of_minus(n, part=whole):
+            if n not in slope_sb:
+                slope_sb[n] = work.tile([P, PACK, WIDE], F32, name="slope", bufs=3)
+            nc.scalar.activation(out=slope_sb[n][part], in_=z_sb[n][part], func=ACT.Gelu_apprx_tanh, scale=-1.0)
 
-        def cubic(n, js):
+        def cubic(n, part=whole):
             if n not in tanh_sb:
-                tanh_sb[n] = work.tile([P, PACK, K_PASS], F32, name="tanh_sb", bufs=2)
+                tanh_sb[n] = work.tile([P, PACK, WIDE], F32, name="tanh", bufs=2)
             nc.vector.scalar_tensor_tensor(
-                out=tanh_sb[n][:, js, :], in0=sq[n][:, js, :], scalar=3.0 * GELU_C, in1=z_sb[n][:, js, :],
+                out=tanh_sb[n][part], in0=square_sb[n][part], scalar=3.0 * GELU_C, in1=z_sb[n][part],
                 op0=ALU.add, op1=ALU.mult,
             )
 
-        def tanh_neg(n, js):
-            nc.scalar.activation(out=tanh_sb[n][:, js, :], in_=tanh_sb[n][:, js, :], func=ACT.Tanh, scale=-1.0 / 3.0)
+        def minus_tanh(n, part=whole):
+            nc.scalar.activation(out=tanh_sb[n][part], in_=tanh_sb[n][part], func=ACT.Tanh, scale=-1.0 / 3.0)
 
-        def slope(n, js):
+        def slope(n, part=whole):
             nc.vector.scalar_tensor_tensor(
-                out=gate[n][:, js, :], in0=sq[n][:, js, :], scalar=GELU_C, in1=gate[n][:, js, :],
+                out=slope_sb[n][part], in0=square_sb[n][part], scalar=GELU_C, in1=slope_sb[n][part],
                 op0=ALU.add, op1=ALU.mult,
             )
 
-        def dh_pass(n, j):
+        def dh_rows(n, rows):
             c, g = divmod(n, HALVES)
-            dh[n, j] = dh_bank()
-            mx_pass(dh[n, j], mx["g", g], E5M2, j, mx["w2", c], E4M3, True, True)
+            for j in rows:
+                dh[n, j] = row_bank()
+                mx_pass(dh[n, j], mx["grad", g], E5M2, j, mx["w2", c], E4M3, True, True)
 
-        def take_dh(n, j):
-            nc.vector.scalar_tensor_tensor(
-                out=tanh_sb[n][:, j, :], in0=tanh_sb[n][:, j, :], scalar=1.0, in1=dh[n, j][:],
-                op0=ALU.subtract, op1=ALU.mult,
-            )
-
-        def round_dz(n, js):
-            if n not in dz:
-                dz[n] = work.tile([P, 2, PACK, 2 * P], BF16, name="dz", bufs=2)
-            for u in range(2):
+        def take_dh(n, rows):
+            for j in rows:
                 nc.vector.scalar_tensor_tensor(
-                    out=dz[n][:, u, js, :].rearrange("p j (m e) -> p (j m) e", e=2),
-                    in0=gate[n][:, js, :].rearrange("p j (m u e) -> p (j m) u e", u=2, e=2)[:, :, u, :],
-                    scalar=0.5,
-                    in1=tanh_sb[n][:, js, :].rearrange("p j (m u e) -> p (j m) u e", u=2, e=2)[:, :, u, :],
+                    out=tanh_sb[n][:, j, :], in0=tanh_sb[n][:, j, :], scalar=1.0, in1=dh[n, j][:],
                     op0=ALU.subtract, op1=ALU.mult,
                 )
 
-        feat_bank, tok_bank = {}, {}
-
-        def turn_dz(n, pair):
-            words = dz[n][:].rearrange("p u j x -> p (u j x)").bitcast(F32)
-            feat_bank[n, pair] = side_bank()
-            turn_words(
-                feat_bank[n, pair],
-                lambda b, u: words[:, (u * PACK + 2 * pair + b) * P : (u * PACK + 2 * pair + b + 1) * P],
-            )
-
-        def weave_dz(n, u):
-            tok_bank[n, u] = psum.tile([P, 2 * K_PASS], BF16, name="side", bufs=SIDE_BANKS)
-            for h in range(2):
-                nc.tensor.matmul(
-                    out=tok_bank[n, u][:, h * K_PASS : (h + 1) * K_PASS].rearrange("p (f j) -> p f j", j=PACK),
-                    lhsT=ident_bf16[:],
-                    rhs=dz[n][:, u, :, h * P : (h + 1) * P].rearrange("p j f -> p f j"),
-                    start=True,
-                    stop=True,
+        def round_dz(n):
+            dz[n] = work.tile([P, 2, PACK, 2 * P], BF16, name="dz", bufs=2)
+            for u in range(2):
+                nc.vector.scalar_tensor_tensor(
+                    out=dz[n][:, u, :, :].rearrange("p j (m e) -> p (j m) e", e=2),
+                    in0=slope_sb[n][:].rearrange("p j (m u e) -> p (j m) u e", u=2, e=2)[:, :, u, :],
+                    scalar=0.5,
+                    in1=tanh_sb[n][:].rearrange("p j (m u e) -> p (j m) u e", u=2, e=2)[:, :, u, :],
+                    op0=ALU.subtract, op1=ALU.mult,
                 )
 
-        def collect_feat(n, pair):
-            if ("feat", n) not in staged_of:
-                staged_of["feat", n] = new_staged("dz_staged", 3)
-            collect_words(nc.scalar.copy, staged_of["feat", n], pair, feat_bank[n, pair])
+        def turn_dz(n):
+            words = dz[n][:].rearrange("p u j x -> p (u j x)").bitcast(F32)
 
-        def collect_tok(n, u):
-            if ("tok", n) not in staged_of:
-                staged_of["tok", n] = new_staged("dz_staged", 3)
-            nc.scalar.copy(out=staged_of["tok", n][:, u * 2 * K_PASS : (u + 1) * 2 * K_PASS], in_=tok_bank[n, u][:])
+            def word_block(pair, b, u):
+                s = u * PACK + 2 * pair + b
+                return words[:, s * P : (s + 1) * P]
 
-        def quantize_feat(n, first, count):
-            if ("feat", n) not in mx:
-                mx["feat", n] = mx_operand(work, "feat", 8)
-            quantize(mx["feat", n], staged_of["feat", n], E5M2, first, count)
+            for pair in range(2):
+                dz_banks[n, "features", pair] = turn_words(partial(word_block, pair))
 
-        def quantize_tok(n):
-            mx["tok", n] = mx_operand(work, "tok", 6)
-            quantize(mx["tok", n], staged_of["tok", n], E5M2)
+        def weave_dz(n):
+            for u in range(2):
+                bank = turn_bank(2 * WIDE, BF16)
+                for h in range(2):
+                    nc.tensor.matmul(
+                        out=bank[:, h * WIDE : (h + 1) * WIDE].rearrange("p (f j) -> p j f", j=PACK),
+                        lhsT=ident_bf16[:],
+                        rhs=dz[n][:, u, :, h * P : (h + 1) * P],
+                        start=True,
+                        stop=True,
+                    )
+                dz_banks[n, "tokens", u] = bank
+
+        def collect_features(n):
+            staged["dz", n] = work.tile([P, 2, PACK * WIDE], BF16, name="dz_staged", bufs=2, align_bytes=64)
+            for pair in range(2):
+                collect_words(nc.scalar.copy, staged["dz", n][:, 0, :], pair, dz_banks[n, "features", pair])
+
+        def collect_tokens(n):
+            for u in range(2):
+                nc.scalar.copy(
+                    out=staged["dz", n][:, 1, u * 2 * WIDE : (u + 1) * 2 * WIDE], in_=dz_banks[n, "tokens", u][:]
+                )
+
+        def quantize_dz(n, first=0, count=2):
+            if ("dz", n) not in mx:
+                codes = keep.tile([P, 2 * WIDE], U32, name="dz%d_codes" % n, align_bytes=64)
+                scales = keep.tile([P, 2 * WIDE], U8, name="dz%d_scales" % n, align_bytes=64)
+                mx["dz", n] = (codes, scales)
+                mx["features", n] = (codes[:, :WIDE], scales[:, :WIDE])
+                mx["tokens", n] = (codes[:, WIDE:], scales[:, WIDE:])
+            codes, scales = mx["dz", n]
+            cols = slice(first * WIDE, (first + count) * WIDE)
+            nc.vector.quantize_mx(
+                out=codes[:, cols].bitcast(E5M2),
+                scales=scales[:, cols],
+                in_=staged["dz", n][:, first : first + count, :].rearrange("p s k -> p (s k)"),
+            )
+
+        def affine_cols_job():
+            def fill():
+                bank = turn_bank(P, BF16)
+                nc.tensor.transpose(bank[:], affine_rows[:], ident_bf16[:])
+                return bank
+
+            return [(fill, lambda bank: nc.scalar.copy(out=affine_cols[:], in_=bank[:, 0 : 2 * PACK]))]
+
+        def gamma_row_job():
+            def fill():
+                bank = turn_bank()
+                for m in range(PACK):
+                    nc.tensor.transpose(
+                        bank[:, m * P : (m + 1) * P], affine_cols[:, m : m + 1].to_broadcast([P, P]), ident_f32[:]
+                    )
+                return bank
+
+            return [(fill, lambda bank: nc.scalar.copy(out=gamma_row[:], in_=bank[:]))]
 
         def normalise(g):
             for j in range(PACK):
@@ -252,11 +276,9 @@ def tile_layernormmlp_v_kernel(
                     op0=ALU.subtract, op1=ALU.mult,
                 )
 
-        ln_t = {}
-
-        def ln_blocks(g):
+        def ln_round_jobs(g):
             def fill(m):
-                bank = side_bank()
+                bank = turn_bank()
                 for j in range(PACK):
                     nc.tensor.transpose(
                         bank[:, j * P : (j + 1) * P], xhat[g][:, j, m * P : (m + 1) * P], ident_f32[:]
@@ -264,7 +286,7 @@ def tile_layernormmlp_v_kernel(
                 return bank
 
             def drain(m, bank):
-                ln_t[g, m] = work.tile([P, K_PASS], BF16, name="ln_t", bufs=4)
+                ln_t[g, m] = work.tile([P, WIDE], BF16, name="ln_t", bufs=PACK)
                 nc.scalar.activation(
                     out=ln_t[g, m][:].rearrange("p (u r e) -> p u r e", u=2, e=2),
                     in_=bank[:].rearrange("p (u e r) -> p u r e", u=2, e=2),
@@ -275,289 +297,215 @@ def tile_layernormmlp_v_kernel(
 
             return [(partial(fill, m), partial(drain, m)) for m in range(PACK)]
 
-        def ln_turns(g):
-            def fill(pair):
-                bank = side_bank()
-                turn_words(bank, lambda b, u: ln_t[g, 2 * pair + b][:].bitcast(F32)[:, u * P : (u + 1) * P])
-                return bank
+        def ln_turn_jobs(g):
+            def word_block(pair, b, u):
+                return ln_t[g, 2 * pair + b][:].bitcast(F32)[:, u * P : (u + 1) * P]
 
-            def drain(pair, bank):
-                if pair == 0:
-                    staged_of["ln", g] = new_staged("side_staged", 2)
-                collect_words(nc.scalar.copy, staged_of["ln", g], pair, bank)
+            return [
+                (
+                    partial(turn_words, partial(word_block, pair)),
+                    partial(collect_operand, ("ln", g), nc.scalar.copy, pair),
+                )
+                for pair in range(2)
+            ]
 
-            return [(partial(fill, pair), partial(drain, pair)) for pair in range(2)]
-
-        def dw_blocks(c):
+        def dw_jobs(c):
             def fill(m):
-                bank = side_bank()
+                bank = turn_bank()
                 for g in range(HALVES):
-                    mx_pass(bank, mx["ln", g], E4M3, m, mx["tok", c * HALVES + g], E5M2, g == 0, g == HALVES - 1)
+                    mx_pass(bank, mx["ln", g], E4M3, m, mx["tokens", c * HALVES + g], E5M2, g == 0, g == HALVES - 1)
                 return bank
 
             def drain(m, bank):
-                dw = work.tile([P, K_PASS], F32, name="dw", bufs=8)
+                dw = work.tile([P, WIDE], F32, name="dw", bufs=5)
                 nc.scalar.copy(
                     out=dw[:].rearrange("p (m u e) -> p m u e", u=2, e=2),
                     in_=bank[:].rearrange("p (u m e) -> p m u e", u=2, e=2),
                 )
-                nc.sync.dma_start(out=out_1[m * P : (m + 1) * P, c * K_PASS : (c + 1) * K_PASS], in_=dw[:])
+                nc.sync.dma_start(out=out_1[m * P : (m + 1) * P, c * WIDE : (c + 1) * WIDE], in_=dw[:])
 
             return [(partial(fill, m), partial(drain, m)) for m in range(PACK)]
 
-        def start_jobs(jobs, lead):
-            return [fill() for fill, drain in jobs[:lead]]
-
-        def finish_jobs(jobs, banks):
-            lead = len(banks)
-            for k, (fill, drain) in enumerate(jobs):
-                drain(banks[k])
-                if k + lead < len(jobs):
-                    banks.append(jobs[k + lead][0]())
-
-        def run_jobs(jobs, lead):
-            finish_jobs(jobs, start_jobs(jobs, lead))
-
-        scaled, dx, scaled_sb, dx_sb = {}, {}, {}, {}
-
-        dln = {}
-
-        def dln_passes(g, j, chunks, bank=None):
-            if (g, j) not in dln:
-                dln[g, j] = bank
-            for c in chunks:
-                mx_pass(dln[g, j], mx["feat", c * HALVES + g], E5M2, j, mx["w1", c], E4M3, c == 0, c == CHUNKS - 1)
-            return dln[g, j]
-
-        def take_dln(g, j, bank):
-            if j == 0:
-                scaled_sb[g] = work.tile([P, PACK, D], F32, name="scaled", tag="sq", bufs=2)
-            scaled[g, j] = scaled_sb[g][:, j, :]
-            nc.vector.scalar_tensor_tensor(
-                out=scaled[g, j], in0=bank[:], scalar=rstd_sb[:, g, j : j + 1], in1=gamma_row[:],
-                op0=ALU.mult, op1=ALU.mult, accum_out=sums[:, g * PACK + j, 0:1],
-            )
-
-        def dln_jobs(g, js):
-            return [(lambda j=j: dln_passes(g, j, range(CHUNKS), side_bank()), partial(take_dln, g, j)) for j in js]
-
-        def dx_moment(g, j):
-            if j == 0:
-                dx_sb[g] = work.tile([P, PACK, D], F32, name="dx", tag="z", bufs=3)
-            dx[g, j] = dx_sb[g][:, j, :]
-            nc.vector.scalar_tensor_tensor(
-                out=dx[g, j], in0=scaled[g, j], scalar=1.0, in1=xhat[g][:, j, :],
-                op0=ALU.mult, op1=ALU.mult, accum_out=sums[:, g * PACK + j, 1:2],
-            )
-
-        def dx_shift(g, j):
-            nc.scalar.activation(
-                out=dx[g, j], in_=xhat[g][:, j, :], func=ACT.Identity,
-                scale=sums[:, g * PACK + j, 1:2], bias=sums[:, g * PACK + j, 0:1],
-            )
-
-        def dx_finish(g, j):
-            nc.vector.scalar_tensor_tensor(
-                out=dx[g, j], in0=dx[g, j], scalar=-1.0 / D, in1=scaled[g, j], op0=ALU.mult, op1=ALU.add
-            )
-            nc.sync.dma_start(out=token_rows(out_0, g)[:, j, :], in_=dx[g, j])
-
-        whole = slice(0, PACK)
-        singles = [slice(j, j + 1) for j in range(PACK)]
-        pairs = [slice(0, 2), slice(2, 4)]
-
-        def affine_jobs():
-            def fill_cols():
-                bank = psum.tile([P, P], BF16, name="side", bufs=SIDE_BANKS)
-                nc.tensor.transpose(bank[:], affine_rows[:], ident_bf16[:])
-                return bank
-
-            def fill_row():
-                bank = side_bank()
-                for m in range(PACK):
-                    nc.tensor.transpose(
-                        bank[:, m * P : (m + 1) * P], affine_cols[:, m : m + 1].to_broadcast([P, P]), ident_f32[:]
+        def dln_rows(g, rows):
+            for j in rows:
+                dln[g, j] = row_bank()
+                for c in range(CHUNKS):
+                    mx_pass(
+                        dln[g, j], mx["features", c * HALVES + g], E5M2, j, mx["w1", c], E4M3,
+                        c == 0, c == CHUNKS - 1,
                     )
-                return bank
 
-            return [
-                (fill_cols, lambda bank: nc.scalar.copy(out=affine_cols[:], in_=bank[:, 0 : 2 * PACK])),
-                (fill_row, lambda bank: nc.scalar.copy(out=gamma_row[:], in_=bank[:])),
-            ]
+        def take_dln(g, rows):
+            if g not in scaled:
+                scaled[g] = work.tile([P, PACK, D], F32, name="scaled", tag="square", bufs=2)
+            for j in rows:
+                nc.vector.scalar_tensor_tensor(
+                    out=scaled[g][:, j, :], in0=dln[g, j][:], scalar=rstd_sb[:, g, j : j + 1], in1=gamma_row[:],
+                    op0=ALU.mult, op1=ALU.mult, accum_out=sums[:, g * PACK + j, 0:1],
+                )
 
-        def dh_bank():
-            return psum.tile([P, K_PASS], F32, name="dh", bufs=DH_BANKS)
+        def dx_correction(g, rows):
+            if g not in dx:
+                dx[g] = work.tile([P, PACK, D], F32, name="dx", tag="z", bufs=3)
+            for j in rows:
+                nc.vector.scalar_tensor_tensor(
+                    out=dx[g][:, j, :], in0=scaled[g][:, j, :], scalar=1.0, in1=xhat[g][:, j, :],
+                    op0=ALU.mult, op1=ALU.mult, accum_out=sums[:, g * PACK + j, 1:2],
+                )
+                nc.scalar.activation(
+                    out=dx[g][:, j, :], in_=xhat[g][:, j, :], func=ACT.Identity,
+                    scale=sums[:, g * PACK + j, 1:2], bias=sums[:, g * PACK + j, 0:1],
+                )
 
+        def dx_finish(g, rows):
+            for j in rows:
+                nc.vector.scalar_tensor_tensor(
+                    out=dx[g][:, j, :], in0=dx[g][:, j, :], scalar=-1.0 / D, in1=scaled[g][:, j, :],
+                    op0=ALU.mult, op1=ALU.add,
+                )
+                nc.sync.dma_start(out=token_rows(out_0, g)[:, j, :], in_=dx[g][:, j, :])
+
+        def piece(first, count=1, cols=slice(0, WIDE)):
+            return (slice(0, P), slice(first, first + count), cols)
+
+        left, right = piece(0, cols=slice(0, WIDE // 2)), piece(0, cols=slice(WIDE // 2, WIDE))
         make_identity(nc, ident_f32[:])
         nc.gpsimd.memset(affine_rows[:], 0.0)
         make_identity(nc, ident_bf16[:])
-        load_z(0, singles[:1])
-        load_grad(0)
-        load_z(0, singles[1:2])
-        load_w2(0)
-        load_z(0, pairs[1:])
-        load_z(1, [whole])
-        load_grad(1)
-        load_x(0)
-        nc.sync.dma_start(out=affine_rows[0:PACK, :], in_=gamma.rearrange("(m p) -> m p", p=P))
-        nc.sync.dma_start(out=affine_rows[PACK : 2 * PACK, :], in_=beta.rearrange("(m p) -> m p", p=P))
+        for part in (left, right, piece(1)):
+            load_z(0, part[1], part[2])
+        load_raw(("grad", 0))
+        for part in (piece(2), piece(3)):
+            load_z(0, part[1], part[2])
+        load_raw(("w2", 0))
+        load_z(1)
+        load_raw(("grad", 1))
+        load_raw(("x", 0))
         nc.sync.dma_start(out=mu_sb[:], in_=mu.rearrange("(g p j) o -> p g (j o)", g=HALVES, j=PACK))
         nc.sync.dma_start(out=rstd_sb[:], in_=rstd.rearrange("(g p j) o -> p g (j o)", g=HALVES, j=PACK))
-        load_z(2, [whole])
+        nc.sync.dma_start(out=affine_rows[0:PACK, :], in_=gamma.rearrange("(m p) -> m p", p=P))
+        nc.sync.dma_start(out=affine_rows[PACK : 2 * PACK, :], in_=beta.rearrange("(m p) -> m p", p=P))
+        load_z(2)
 
-        head_jobs = turn_raw(("g", 0), nc.vector.tensor_copy) + turn_raw(("w2", 0), nc.vector.tensor_copy)
-        banks = start_jobs(head_jobs, 4)
-        gelu_neg(0, singles[0])
-        for js in singles[:2]:
-            square(0, js)
-            cubic(0, js)
-        gelu_neg(0, singles[1])
-        finish_jobs(head_jobs[:2], banks[:2])
-        square(0, pairs[1])
-        tanh_neg(0, pairs[0])
-        cubic(0, pairs[1])
-        gelu_neg(0, pairs[1])
-        tanh_neg(0, pairs[1])
-        finish_jobs(head_jobs[2:], banks[2:])
-        quantize_raw(("g", 0), E5M2)
-        quantize_raw(("w2", 0), E4M3)
-        slope(0, whole)
-        square(1, whole)
-        for j in range(DH_BANKS):
-            dh_pass(0, j)
+        jobs = operand_jobs(("grad", 0), nc.vector.tensor_copy) + operand_jobs(("w2", 0), nc.vector.tensor_copy)
+        banks = fill_jobs(jobs)
+        gelu_of_minus(0, left)
+        for part in (left, right, piece(1)):
+            square(0, part)
+            cubic(0, part)
+        gelu_of_minus(0, right)
+        gelu_of_minus(0, piece(1))
+        slope(0, piece(0))
+        drain_jobs(jobs[0:1], banks[0:1])
+        for part in (piece(2), piece(3)):
+            square(0, part)
+            cubic(0, part)
+        drain_jobs(jobs[1:2], banks[1:2])
+        minus_tanh(0, piece(0, 2))
+        gelu_of_minus(0, piece(2, 2))
+        slope(0, piece(1))
+        drain_jobs(jobs[2:3], banks[2:3])
+        quantize_operand(("grad", 0))
+        drain_jobs(jobs[3:4], banks[3:4])
+        square(1)
+        minus_tanh(0, piece(2, 2))
+        slope(0, piece(2))
+        quantize_operand(("w2", 0))
+        slope(0, piece(3))
+        dh_rows(0, range(PACK))
+        load_raw(("w2", 1))
+        load_raw(("w1", 0))
 
-        loads = {
-            -1: [partial(load_w1, 0), partial(load_w1, 1), partial(load_w2, 1)],
-            0: [partial(load_w1, 2)],
-            1: [partial(load_w2, 2), partial(load_w1, 3)],
-            2: [partial(load_x, 1)],
-            3: [partial(load_w2, 3)],
-        }
         operands = {
-            0: [(("g", 1), E5M2), (("w1", 0), E4M3)],
-            1: [(("w2", 1), E4M3)],
-            2: [(("w1", 1), E4M3)],
-            3: [(("w2", 2), E4M3), (("w1", 2), E4M3)],
-            4: [(("w1", 3), E4M3)],
-            5: [(("w2", 3), E4M3)],
+            0: [("grad", 1), ("w2", 1), ("w1", 0)],
+            2: [("w2", 2)],
+            3: [("w1", 1), ("w1", 2)],
+            4: [("w2", 3)],
+            5: [("w1", 3)],
         }
-        for step in loads[-1]:
-            step()
-
-        for n in range(UNITS - 1):
-            jobs = []
-            if n == 0:
-                jobs = jobs + affine_jobs()[:1]
-            if n == 6:
-                jobs = jobs + affine_jobs()[1:]
-            for key, fmt in operands.get(n, []):
-                jobs = jobs + turn_raw(key, nc.scalar.copy)
-            if n in (2, 5):
-                jobs = jobs + ln_turns(n // 3)
-            if n in (1, 4):
-                jobs = jobs + ln_blocks(n // 3)
-            if n == 6:
-                jobs = jobs + dw_blocks(0) + dw_blocks(1)
-            gelu_neg(n + 1, whole)
-            cubic(n + 1, whole)
+        normalise_at = {0: 0, 3: 1}
+        last = UNITS - 1
+        for n in range(last):
+            jobs = affine_cols_job() if n == 0 else []
+            for key in operands.get(n, []):
+                jobs = jobs + operand_jobs(key, nc.scalar.copy)
+            if n - 2 in normalise_at:
+                jobs = jobs + ln_turn_jobs(normalise_at[n - 2])
+            if n - 1 in normalise_at:
+                jobs = jobs + ln_round_jobs(normalise_at[n - 1])
+            if n == last - 1:
+                jobs = gamma_row_job() + dw_jobs(0)
+            gelu_of_minus(n + 1)
+            cubic(n + 1)
             if n + 3 < UNITS:
-                load_z(n + 3, [whole])
-            banks = start_jobs(jobs, EARLY)
-            take_dh(n, 0)
-            for j in range(DH_BANKS, PACK):
-                dh_pass(n, j)
+                load_z(n + 3)
+            banks = fill_jobs(jobs[:2])
             if n > 0:
-                for k in range(2):
-                    collect_tok(n - 1, k)
-            banks = banks + start_jobs(jobs[EARLY:], SIDE_BANKS - EARLY)
-            for j in range(1, PACK):
-                take_dh(n, j)
-            tanh_neg(n + 1, whole)
-            finish_jobs(jobs, banks)
+                collect_tokens(n - 1)
+            banks = banks + fill_jobs(jobs[2:TURN_BANKS])
+            take_dh(n, range(PACK))
             if n > 0:
-                quantize_feat(n - 1, 0, PACK)
-                quantize_tok(n - 1)
-            ready = ("g", (n + 1) % HALVES) in mx and ("w2", (n + 1) // HALVES) in mx
-            if ready:
-                for j in range(DH_BANKS):
-                    dh_pass(n + 1, j)
-            round_dz(n, whole)
-            for k in range(2):
-                turn_dz(n, k)
-            for k in range(2):
-                weave_dz(n, k)
+                dh_rows(n + 1, range(2))
+            minus_tanh(n + 1)
+            drain_jobs(jobs, banks)
+            if n > 0:
+                dh_rows(n + 1, range(2, PACK))
+                quantize_dz(n - 1)
+            if n in normalise_at:
+                normalise(normalise_at[n])
+            round_dz(n)
+            turn_dz(n)
+            if n == 0:
+                quantize_operand(("grad", 1))
+                dh_rows(1, range(PACK))
+            weave_dz(n)
             if n + 2 < UNITS:
-                square(n + 2, whole)
-            for key, fmt in operands.get(n, []):
-                quantize_raw(key, fmt)
-            if n in (2, 5):
-                quantize_raw(("ln", n // 3), E4M3)
-            slope(n + 1, whole)
-            if n in (0, 3):
-                normalise(n // 3)
-            if not ready:
-                for j in range(DH_BANKS):
-                    dh_pass(n + 1, j)
-            for k in range(2):
-                collect_feat(n, k)
-            for step in loads.get(n, []):
-                step()
+                square(n + 2)
+            slope(n + 1)
+            for key in operands.get(n, []):
+                if key not in mx:
+                    quantize_operand(key)
+            if n - 2 in normalise_at:
+                quantize_operand(("ln", normalise_at[n - 2]))
+            collect_features(n)
+            for key in operands.get(n + 1, []):
+                load_raw(key)
+            if n + 1 in normalise_at:
+                load_raw(("x", normalise_at[n + 1]))
 
-        n = UNITS - 1
-        take_dh(n, 0)
-        for j in range(DH_BANKS, PACK):
-            dh_pass(n, j)
-        for k in range(2):
-            collect_tok(n - 1, k)
-        take_dh(n, 1)
-        quantize_feat(n - 1, 0, PACK)
-        take_dh(n, 2)
-        take_dh(n, 3)
-        quantize_tok(n - 1)
-        for j in range(DH_BANKS):
-            dln_passes(0, j, range(CHUNKS), dh_bank())
-        round_dz(n, whole)
-        for k in range(2):
-            turn_dz(n, k)
-        dln_passes(0, 3, range(CHUNKS), side_bank())
-        for k in range(2):
-            weave_dz(n, k)
-        for k in range(2):
-            collect_feat(n, k)
-        for k in range(2):
-            collect_tok(n, k)
-        for j in range(PACK):
-            take_dln(0, j, dln[0, j])
-        jobs = dw_blocks(2) + dw_blocks(3)
-        banks = start_jobs(jobs[:4], 4)
-        quantize_feat(n, 0, PACK)
-        for j in range(DH_BANKS):
-            dln_passes(1, j, range(CHUNKS), dh_bank())
-        for j in range(2):
-            dx_moment(0, j)
-            dx_shift(0, j)
-        quantize_tok(n)
-        finish_jobs(jobs[:2], banks[:2])
-        for j in range(2, 4):
-            dx_moment(0, j)
-            dx_shift(0, j)
-        finish_jobs(jobs[2:4], banks[2:])
-        banks = start_jobs(jobs[4:], 4)
-        dx_finish(0, 0)
-        dx_finish(0, 1)
-        take_dln(1, 0, dln[1, 0])
-        dln_passes(1, 3, range(CHUNKS), dh_bank())
-        take_dln(1, 1, dln[1, 1])
-        finish_jobs(jobs[4:], banks)
-        dx_finish(0, 2)
-        dx_finish(0, 3)
-        for j in range(2):
-            dx_moment(1, j)
-            dx_shift(1, j)
-        for j in range(2, 4):
-            take_dln(1, j, dln[1, j])
-        for j in range(2, 4):
-            dx_moment(1, j)
-            dx_shift(1, j)
-        for j in range(PACK):
-            dx_finish(1, j)
+        take_dh(last, [0])
+        collect_tokens(last - 1)
+        jobs = dw_jobs(1)
+        drain_jobs(jobs, fill_jobs(jobs))
+        take_dh(last, [1, 2])
+        quantize_dz(last - 1, 0, 1)
+        take_dh(last, [3])
+        dln_rows(0, range(3))
+        quantize_dz(last - 1, 1, 1)
+        round_dz(last)
+        turn_dz(last)
+        dln_rows(0, [3])
+        weave_dz(last)
+        collect_features(last)
+        take_dln(0, range(3))
+        dx_correction(0, [0, 1])
+        collect_tokens(last)
+        take_dln(0, [3])
+        quantize_dz(last, 0, 1)
+        dln_rows(1, [0, 1])
+        jobs = dw_jobs(2)
+        banks = fill_jobs(jobs)
+        dln_rows(1, [2, 3])
+        dx_correction(0, [2, 3])
+        quantize_dz(last, 1, 1)
+        dx_finish(0, [0, 1])
+        drain_jobs(jobs, banks)
+        jobs = dw_jobs(3)
+        banks = fill_jobs(jobs)
+        take_dln(1, [0, 1])
+        dx_finish(0, [2, 3])
+        dx_correction(1, [0, 1])
+        drain_jobs(jobs, banks)
+        take_dln(1, [2, 3])
+        dx_correction(1, [2, 3])
+        dx_finish(1, range(PACK))

import math
from contextlib import ExitStack
from functools import partial

import concourse.mybir as mybir
from concourse.masks import make_identity

T, D, F1, F2 = 1024, 512, 2048, 512
FLOPS = 2 * T * F2 * F1 + 2 * T * F1 * D + 2 * T * D * F1
BYTES = 2 * (T * D + 2 * D + D * F1 + F1 * F2 + T * F2) + 4 * (2 * T + T * F1 + T * D + D * F1)

F32 = mybir.dt.float32
BF16 = mybir.dt.bfloat16
U32 = mybir.dt.uint32
U8 = mybir.dt.uint8
E4M3 = mybir.dt.float8_e4m3fn_x4
E5M2 = mybir.dt.float8_e5m2_x4
ALU = mybir.AluOpType
ACT = mybir.ActivationFunctionType

P = 128
PACK = 4
WIDE = P * PACK
HALVES = T // WIDE
CHUNKS = F1 // WIDE
UNITS = HALVES * CHUNKS
GELU_C = 0.7978845608028654
GELU_A = 0.044715
ROW_BANKS = 4
TURN_BANKS = 4


def tile_layernormmlp_v_kernel(
    tc, inputs, gamma, beta, fc1_kernel, fc1_bias, fc2_kernel, fc2_bias, mu, rstd, z1, grad_out, out_0, out_1
):
    nc = tc.nc
    with ExitStack() as ctx:
        keep = ctx.enter_context(tc.tile_pool(name="keep", bufs=1))
        work = ctx.enter_context(tc.tile_pool(name="work", bufs=2))
        psum = ctx.enter_context(tc.psum_pool(name="psum", bufs=ROW_BANKS))
        ctx.enter_context(tc.manual_schedule())

        ident_f32 = keep.tile([P, P], F32)
        ident_bf16 = keep.tile([P, P], BF16)
        affine_rows = keep.tile([P, P], BF16)
        affine_cols = keep.tile([P, 2 * PACK], F32)
        gamma_row = keep.tile([P, D], F32)
        mu_sb = keep.tile([P, HALVES, PACK], F32)
        rstd_sb = keep.tile([P, HALVES, PACK], F32)
        sums = keep.tile([P, HALVES * PACK, 2], F32)
        xhat = [keep.tile([P, PACK, D], F32, name="xhat%d" % g) for g in range(HALVES)]

        raw, staged, mx = {}, {}, {}
        z_sb, square_sb, slope_sb, tanh_sb, dh, dz, dz_banks = {}, {}, {}, {}, {}, {}, {}
        ln_t, dln, scaled, dx = {}, {}, {}, {}

        def row_bank():
            return psum.tile([P, WIDE], F32, name="row_bank", bufs=ROW_BANKS)

        def turn_bank(width=WIDE, dtype=F32):
            return psum.tile([P, width], dtype, name="turn_bank", bufs=TURN_BANKS)

        def mx_pass(bank, still, still_fmt, block, moving, moving_fmt, start, stop):
            cols = slice(block * P, (block + 1) * P)
            nc.tensor.matmul_mx(
                out=bank[:],
                lhsT=still[0][:, cols].bitcast(still_fmt),
                lhsT_scale=still[1][:, cols],
                rhs=moving[0].bitcast(moving_fmt),
                rhs_scale=moving[1],
                start=start,
                stop=stop,
            )

        def turn_words(word_block):
            bank = turn_bank()
            for b in range(2):
                for u in range(2):
                    s = 2 * b + u
                    nc.tensor.transpose(bank[:, s * P : (s + 1) * P], word_block(b, u), ident_f32[:])
            return bank

        def collect_words(copy, target, pair, bank):
            words = target.bitcast(F32)[:, pair * WIDE : (pair + 1) * WIDE]
            copy(
                out=words.rearrange("p (b r u) -> p b r u", b=2, u=2),
                in_=bank[:].rearrange("p (b u r) -> p b r u", b=2, u=2),
            )

        def fill_jobs(jobs):
            return [fill() for fill, drain in jobs]

        def drain_jobs(jobs, banks):
            banks = list(banks)
            for k, (fill, drain) in enumerate(jobs):
                drain(banks[k])
                if len(banks) < len(jobs):
                    banks.append(jobs[len(banks)][0]())

        def token_rows(src, g):
            return src[g * WIDE : (g + 1) * WIDE, :].rearrange("(p j) w -> p j w", j=PACK)

        def load_raw(key):
            kind, i = key
            cut = slice(i * WIDE, (i + 1) * WIDE)
            if kind == "grad":
                rows = token_rows(grad_out, i)
            elif kind == "x":
                rows = token_rows(inputs, i)
            elif kind == "w2":
                rows = fc2_kernel[cut, :].rearrange("(m p) k -> p m k", p=P)
            else:
                rows = fc1_kernel[:, cut].rearrange("(m p) k -> p m k", p=P)
            raw[key] = work.tile([P, PACK, WIDE], BF16, name="raw", bufs=4)
            nc.sync.dma_start(out=raw[key][:], in_=rows)

        def load_z(n, rows=slice(0, PACK), cols=slice(0, WIDE)):
            c, g = divmod(n, HALVES)
            if n not in z_sb:
                z_sb[n] = work.tile([P, PACK, WIDE], F32, name="z", tag="z", bufs=3)
            unit = token_rows(z1, g)[:, :, c * WIDE : (c + 1) * WIDE]
            nc.sync.dma_start(out=z_sb[n][:, rows, cols], in_=unit[:, rows, cols])

        def collect_operand(key, copy, pair, bank):
            if pair == 0:
                staged[key] = work.tile([P, PACK * WIDE], BF16, name="staged", bufs=3, align_bytes=64)
            collect_words(copy, staged[key][:], pair, bank)

        def operand_jobs(key, copy):
            words = raw[key][:].rearrange("p m k -> p (m k)").bitcast(F32)

            def word_block(pair, b, u):
                row = 2 * pair + b
                return words[:, row * 2 * P + u : (row + 1) * 2 * P : 2]

            return [
                (partial(turn_words, partial(word_block, pair)), partial(collect_operand, key, copy, pair))
                for pair in range(2)
            ]

        def quantize_operand(key):
            codes = keep.tile([P, WIDE], U32, name="%s%d_codes" % key, align_bytes=64)
            scales = keep.tile([P, WIDE], U8, name="%s%d_scales" % key, align_bytes=64)
            mx[key] = (codes[:], scales[:])
            fmt = E5M2 if key[0] == "grad" else E4M3
            nc.vector.quantize_mx(out=codes[:].bitcast(fmt), scales=scales[:], in_=staged[key][:])

        whole = (slice(0, P), slice(0, PACK), slice(0, WIDE))

        def square(n, part=whole):
            if n not in square_sb:
                square_sb[n] = work.tile([P, PACK, WIDE], F32, name="square", tag="square", bufs=2)
            nc.scalar.activation(
                out=square_sb[n][part], in_=z_sb[n][part], func=ACT.Square, scale=math.sqrt(3.0 * GELU_A * GELU_C)
            )

        def gelu_of_minus(n, part=whole):
            if n not in slope_sb:
                slope_sb[n] = work.tile([P, PACK, WIDE], F32, name="slope", bufs=3)
            nc.scalar.activation(out=slope_sb[n][part], in_=z_sb[n][part], func=ACT.Gelu_apprx_tanh, scale=-1.0)

        def cubic(n, part=whole):
            if n not in tanh_sb:
                tanh_sb[n] = work.tile([P, PACK, WIDE], F32, name="tanh", bufs=2)
            nc.vector.scalar_tensor_tensor(
                out=tanh_sb[n][part], in0=square_sb[n][part], scalar=3.0 * GELU_C, in1=z_sb[n][part],
                op0=ALU.add, op1=ALU.mult,
            )

        def minus_tanh(n, part=whole):
            nc.scalar.activation(out=tanh_sb[n][part], in_=tanh_sb[n][part], func=ACT.Tanh, scale=-1.0 / 3.0)

        def slope(n, part=whole):
            nc.vector.scalar_tensor_tensor(
                out=slope_sb[n][part], in0=square_sb[n][part], scalar=GELU_C, in1=slope_sb[n][part],
                op0=ALU.add, op1=ALU.mult,
            )

        def dh_rows(n, rows):
            c, g = divmod(n, HALVES)
            for j in rows:
                dh[n, j] = row_bank()
                mx_pass(dh[n, j], mx["grad", g], E5M2, j, mx["w2", c], E4M3, True, True)

        def take_dh(n, rows):
            for j in rows:
                nc.vector.scalar_tensor_tensor(
                    out=tanh_sb[n][:, j, :], in0=tanh_sb[n][:, j, :], scalar=1.0, in1=dh[n, j][:],
                    op0=ALU.subtract, op1=ALU.mult,
                )

        def round_dz(n):
            dz[n] = work.tile([P, 2, PACK, 2 * P], BF16, name="dz", bufs=2)
            for u in range(2):
                nc.vector.scalar_tensor_tensor(
                    out=dz[n][:, u, :, :].rearrange("p j (m e) -> p (j m) e", e=2),
                    in0=slope_sb[n][:].rearrange("p j (m u e) -> p (j m) u e", u=2, e=2)[:, :, u, :],
                    scalar=0.5,
                    in1=tanh_sb[n][:].rearrange("p j (m u e) -> p (j m) u e", u=2, e=2)[:, :, u, :],
                    op0=ALU.subtract, op1=ALU.mult,
                )

        def turn_dz(n):
            words = dz[n][:].rearrange("p u j x -> p (u j x)").bitcast(F32)

            def word_block(pair, b, u):
                s = u * PACK + 2 * pair + b
                return words[:, s * P : (s + 1) * P]

            for pair in range(2):
                dz_banks[n, "features", pair] = turn_words(partial(word_block, pair))

        def weave_dz(n):
            for u in range(2):
                bank = turn_bank(2 * WIDE, BF16)
                for h in range(2):
                    nc.tensor.matmul(
                        out=bank[:, h * WIDE : (h + 1) * WIDE].rearrange("p (f j) -> p j f", j=PACK),
                        lhsT=ident_bf16[:],
                        rhs=dz[n][:, u, :, h * P : (h + 1) * P],
                        start=True,
                        stop=True,
                    )
                dz_banks[n, "tokens", u] = bank

        def collect_features(n):
            staged["dz", n] = work.tile([P, 2, PACK * WIDE], BF16, name="dz_staged", bufs=2, align_bytes=64)
            for pair in range(2):
                collect_words(nc.scalar.copy, staged["dz", n][:, 0, :], pair, dz_banks[n, "features", pair])

        def collect_tokens(n):
            for u in range(2):
                nc.scalar.copy(
                    out=staged["dz", n][:, 1, u * 2 * WIDE : (u + 1) * 2 * WIDE], in_=dz_banks[n, "tokens", u][:]
                )

        def quantize_dz(n, first=0, count=2):
            if ("dz", n) not in mx:
                codes = keep.tile([P, 2 * WIDE], U32, name="dz%d_codes" % n, align_bytes=64)
                scales = keep.tile([P, 2 * WIDE], U8, name="dz%d_scales" % n, align_bytes=64)
                mx["dz", n] = (codes, scales)
                mx["features", n] = (codes[:, :WIDE], scales[:, :WIDE])
                mx["tokens", n] = (codes[:, WIDE:], scales[:, WIDE:])
            codes, scales = mx["dz", n]
            cols = slice(first * WIDE, (first + count) * WIDE)
            nc.vector.quantize_mx(
                out=codes[:, cols].bitcast(E5M2),
                scales=scales[:, cols],
                in_=staged["dz", n][:, first : first + count, :].rearrange("p s k -> p (s k)"),
            )

        def affine_cols_job():
            def fill():
                bank = turn_bank(P, BF16)
                nc.tensor.transpose(bank[:], affine_rows[:], ident_bf16[:])
                return bank

            return [(fill, lambda bank: nc.scalar.copy(out=affine_cols[:], in_=bank[:, 0 : 2 * PACK]))]

        def gamma_row_job():
            def fill():
                bank = turn_bank()
                for m in range(PACK):
                    nc.tensor.transpose(
                        bank[:, m * P : (m + 1) * P], affine_cols[:, m : m + 1].to_broadcast([P, P]), ident_f32[:]
                    )
                return bank

            return [(fill, lambda bank: nc.scalar.copy(out=gamma_row[:], in_=bank[:]))]

        def normalise(g):
            for j in range(PACK):
                nc.vector.tensor_scalar(
                    out=xhat[g][:, j, :], in0=raw["x", g][:, j, :],
                    scalar1=mu_sb[:, g, j : j + 1], scalar2=rstd_sb[:, g, j : j + 1],
                    op0=ALU.subtract, op1=ALU.mult,
                )

        def ln_round_jobs(g):
            def fill(m):
                bank = turn_bank()
                for j in range(PACK):
                    nc.tensor.transpose(
                        bank[:, j * P : (j + 1) * P], xhat[g][:, j, m * P : (m + 1) * P], ident_f32[:]
                    )
                return bank

            def drain(m, bank):
                ln_t[g, m] = work.tile([P, WIDE], BF16, name="ln_t", bufs=PACK)
                nc.scalar.activation(
                    out=ln_t[g, m][:].rearrange("p (u r e) -> p u r e", u=2, e=2),
                    in_=bank[:].rearrange("p (u e r) -> p u r e", u=2, e=2),
                    func=ACT.Identity,
                    scale=affine_cols[:, m : m + 1],
                    bias=affine_cols[:, PACK + m : PACK + m + 1],
                )

            return [(partial(fill, m), partial(drain, m)) for m in range(PACK)]

        def ln_turn_jobs(g):
            def word_block(pair, b, u):
                return ln_t[g, 2 * pair + b][:].bitcast(F32)[:, u * P : (u + 1) * P]

            return [
                (
                    partial(turn_words, partial(word_block, pair)),
                    partial(collect_operand, ("ln", g), nc.scalar.copy, pair),
                )
                for pair in range(2)
            ]

        def dw_jobs(c):
            def fill(m):
                bank = turn_bank()
                for g in range(HALVES):
                    mx_pass(bank, mx["ln", g], E4M3, m, mx["tokens", c * HALVES + g], E5M2, g == 0, g == HALVES - 1)
                return bank

            def drain(m, bank):
                dw = work.tile([P, WIDE], F32, name="dw", bufs=5)
                nc.scalar.copy(
                    out=dw[:].rearrange("p (m u e) -> p m u e", u=2, e=2),
                    in_=bank[:].rearrange("p (u m e) -> p m u e", u=2, e=2),
                )
                nc.sync.dma_start(out=out_1[m * P : (m + 1) * P, c * WIDE : (c + 1) * WIDE], in_=dw[:])

            return [(partial(fill, m), partial(drain, m)) for m in range(PACK)]

        def dln_rows(g, rows):
            for j in rows:
                dln[g, j] = row_bank()
                for c in range(CHUNKS):
                    mx_pass(
                        dln[g, j], mx["features", c * HALVES + g], E5M2, j, mx["w1", c], E4M3,
                        c == 0, c == CHUNKS - 1,
                    )

        def take_dln(g, rows):
            if g not in scaled:
                scaled[g] = work.tile([P, PACK, D], F32, name="scaled", tag="square", bufs=2)
            for j in rows:
                nc.vector.scalar_tensor_tensor(
                    out=scaled[g][:, j, :], in0=dln[g, j][:], scalar=rstd_sb[:, g, j : j + 1], in1=gamma_row[:],
                    op0=ALU.mult, op1=ALU.mult, accum_out=sums[:, g * PACK + j, 0:1],
                )

        def dx_correction(g, rows):
            if g not in dx:
                dx[g] = work.tile([P, PACK, D], F32, name="dx", tag="z", bufs=3)
            for j in rows:
                nc.vector.scalar_tensor_tensor(
                    out=dx[g][:, j, :], in0=scaled[g][:, j, :], scalar=1.0, in1=xhat[g][:, j, :],
                    op0=ALU.mult, op1=ALU.mult, accum_out=sums[:, g * PACK + j, 1:2],
                )
                nc.scalar.activation(
                    out=dx[g][:, j, :], in_=xhat[g][:, j, :], func=ACT.Identity,
                    scale=sums[:, g * PACK + j, 1:2], bias=sums[:, g * PACK + j, 0:1],
                )

        def dx_finish(g, rows):
            for j in rows:
                nc.vector.scalar_tensor_tensor(
                    out=dx[g][:, j, :], in0=dx[g][:, j, :], scalar=-1.0 / D, in1=scaled[g][:, j, :],
                    op0=ALU.mult, op1=ALU.add,
                )
                nc.sync.dma_start(out=token_rows(out_0, g)[:, j, :], in_=dx[g][:, j, :])

        def piece(first, count=1, cols=slice(0, WIDE)):
            return (slice(0, P), slice(first, first + count), cols)

        left, right = piece(0, cols=slice(0, WIDE // 2)), piece(0, cols=slice(WIDE // 2, WIDE))
        make_identity(nc, ident_f32[:])
        nc.gpsimd.memset(affine_rows[:], 0.0)
        make_identity(nc, ident_bf16[:])
        for part in (left, right, piece(1)):
            load_z(0, part[1], part[2])
        load_raw(("grad", 0))
        for part in (piece(2), piece(3)):
            load_z(0, part[1], part[2])
        load_raw(("w2", 0))
        load_z(1)
        load_raw(("grad", 1))
        load_raw(("x", 0))
        nc.sync.dma_start(out=mu_sb[:], in_=mu.rearrange("(g p j) o -> p g (j o)", g=HALVES, j=PACK))
        nc.sync.dma_start(out=rstd_sb[:], in_=rstd.rearrange("(g p j) o -> p g (j o)", g=HALVES, j=PACK))
        nc.sync.dma_start(out=affine_rows[0:PACK, :], in_=gamma.rearrange("(m p) -> m p", p=P))
        nc.sync.dma_start(out=affine_rows[PACK : 2 * PACK, :], in_=beta.rearrange("(m p) -> m p", p=P))
        load_z(2)

        jobs = operand_jobs(("grad", 0), nc.vector.tensor_copy) + operand_jobs(("w2", 0), nc.vector.tensor_copy)
        banks = fill_jobs(jobs)
        gelu_of_minus(0, left)
        for part in (left, right, piece(1)):
            square(0, part)
            cubic(0, part)
        gelu_of_minus(0, right)
        gelu_of_minus(0, piece(1))
        slope(0, piece(0))
        drain_jobs(jobs[0:1], banks[0:1])
        for part in (piece(2), piece(3)):
            square(0, part)
            cubic(0, part)
        drain_jobs(jobs[1:2], banks[1:2])
        minus_tanh(0, piece(0, 2))
        gelu_of_minus(0, piece(2, 2))
        slope(0, piece(1))
        drain_jobs(jobs[2:3], banks[2:3])
        quantize_operand(("grad", 0))
        drain_jobs(jobs[3:4], banks[3:4])
        square(1)
        minus_tanh(0, piece(2, 2))
        slope(0, piece(2))
        quantize_operand(("w2", 0))
        slope(0, piece(3))
        dh_rows(0, range(PACK))
        load_raw(("w2", 1))
        load_raw(("w1", 0))

        operands = {
            0: [("grad", 1), ("w2", 1), ("w1", 0)],
            2: [("w2", 2)],
            3: [("w1", 1), ("w1", 2)],
            4: [("w2", 3)],
            5: [("w1", 3)],
        }
        normalise_at = {0: 0, 3: 1}
        last = UNITS - 1
        for n in range(last):
            jobs = affine_cols_job() if n == 0 else []
            for key in operands.get(n, []):
                jobs = jobs + operand_jobs(key, nc.scalar.copy)
            if n - 2 in normalise_at:
                jobs = jobs + ln_turn_jobs(normalise_at[n - 2])
            if n - 1 in normalise_at:
                jobs = jobs + ln_round_jobs(normalise_at[n - 1])
            if n == last - 1:
                jobs = gamma_row_job() + dw_jobs(0)
            gelu_of_minus(n + 1)
            cubic(n + 1)
            if n + 3 < UNITS:
                load_z(n + 3)
            banks = fill_jobs(jobs[:2])
            if n > 0:
                collect_tokens(n - 1)
            banks = banks + fill_jobs(jobs[2:TURN_BANKS])
            take_dh(n, range(PACK))
            if n > 0:
                dh_rows(n + 1, range(2))
            minus_tanh(n + 1)
            drain_jobs(jobs, banks)
            if n > 0:
                dh_rows(n + 1, range(2, PACK))
                quantize_dz(n - 1)
            if n in normalise_at:
                normalise(normalise_at[n])
            round_dz(n)
            turn_dz(n)
            if n == 0:
                quantize_operand(("grad", 1))
                dh_rows(1, range(PACK))
            weave_dz(n)
            if n + 2 < UNITS:
                square(n + 2)
            slope(n + 1)
            for key in operands.get(n, []):
                if key not in mx:
                    quantize_operand(key)
            if n - 2 in normalise_at:
                quantize_operand(("ln", normalise_at[n - 2]))
            collect_features(n)
            for key in operands.get(n + 1, []):
                load_raw(key)
            if n + 1 in normalise_at:
                load_raw(("x", normalise_at[n + 1]))

        take_dh(last, [0])
        collect_tokens(last - 1)
        jobs = dw_jobs(1)
        drain_jobs(jobs, fill_jobs(jobs))
        take_dh(last, [1, 2])
        quantize_dz(last - 1, 0, 1)
        take_dh(last, [3])
        dln_rows(0, range(3))
        quantize_dz(last - 1, 1, 1)
        round_dz(last)
        turn_dz(last)
        dln_rows(0, [3])
        weave_dz(last)
        collect_features(last)
        take_dln(0, range(3))
        dx_correction(0, [0, 1])
        collect_tokens(last)
        take_dln(0, [3])
        quantize_dz(last, 0, 1)
        dln_rows(1, [0, 1])
        jobs = dw_jobs(2)
        banks = fill_jobs(jobs)
        dln_rows(1, [2, 3])
        dx_correction(0, [2, 3])
        quantize_dz(last, 1, 1)
        dx_finish(0, [0, 1])
        drain_jobs(jobs, banks)
        jobs = dw_jobs(3)
        banks = fill_jobs(jobs)
        take_dln(1, [0, 1])
        dx_finish(0, [2, 3])
        dx_correction(1, [0, 1])
        drain_jobs(jobs, banks)
        take_dln(1, [2, 3])
        dx_correction(1, [2, 3])
        dx_finish(1, range(PACK))
